import numpy as np
import ml_dtypes


def mxq(x, axis, fmt="e4m3"):
    dtype, down = {"e4m3": (ml_dtypes.float8_e4m3fn, 7), "e5m2": (ml_dtypes.float8_e5m2, 14)}[fmt]
    v = np.moveaxis(np.asarray(x, np.float32).astype(ml_dtypes.bfloat16).astype(np.float64), axis, -1)
    blocks = v.reshape(v.shape[:-1] + (-1, 32))
    amax = np.abs(blocks).max(-1, keepdims=True)
    byte = np.maximum(np.where(amax > 0, np.frexp(amax)[1] - 1 + 127, 0) - down, 1)
    scale = np.exp2(byte - 127.0)
    codes = (blocks / scale).astype(np.float32).astype(dtype).astype(np.float64)
    return np.moveaxis((codes * scale).reshape(v.shape), -1, axis)


WIDE = False


def mx_kscale(k):
    if not WIDE:
        return np.ones(k)
    levels = np.array([10, -10, 5, -5, 0])
    a = np.random.permutation(np.resize(levels, k // 512 * 4)).reshape(k // 512, 4)
    idx = np.arange(k)
    return np.exp2(a[idx // 512, idx % 128 // 32])


BF16 = ml_dtypes.bfloat16


def bf(x):
    return np.asarray(x, np.float32).astype(BF16)


def f64(x):
    return np.asarray(x).astype(np.float64)


N, M, J, DIN, D, G = 6144, 1024, 512, 256, 128, 2
QS, KC, KN, CS, VS = 1.5, 1.0, 0.2, 1.0, 8.0
EPS = 1e-9


def elu(r):
    return np.where(r > 0.0, r, np.exp(np.minimum(r, 0.0)) - 1.0)


def setup_inputs():
    s = mx_kscale(M)
    g = np.random.randint(G, size=M)
    q = np.random.standard_normal((N, D)) * QS
    q[:, 0] = QS
    k = np.random.standard_normal((G, D))[g] * KC + np.random.standard_normal((M, D)) * KN
    k[:, 0] += np.log(s) * np.sqrt(D) / QS
    profile = np.exp(CS * np.random.standard_normal((G, J)) - CS * CS / 2.0)
    c = profile[g] * (0.75 + 0.5 * np.random.random((M, J))) / s[:, None]
    v = np.random.standard_normal((J, D)) * VS
    return {"q": bf(q), "k": bf(k), "counting_attn": bf(c), "v": bf(v)}


def reference(q, k, counting_attn, v):
    logits = (f64(q) @ f64(k).T) * (1.0 / np.sqrt(D))
    logits = logits - logits.max(axis=1, keepdims=True)
    e = np.exp(logits)
    a_nomi = mxq(e, 1, "e4m3") @ mxq(f64(counting_attn), 0, "e4m3")
    a_deno = a_nomi.sum(axis=1, keepdims=True)
    a_nor = a_nomi / (a_deno + EPS)
    ret = mxq(a_nor, 1, "e4m3") @ mxq(f64(v), 0, "e4m3")
    return elu(ret)

@@ -1,0 +1,311 @@
+from contextlib import ExitStack
+
+import concourse.mybir as mybir
+from concourse.masks import make_identity
+
+BF16 = mybir.dt.bfloat16
+F32 = mybir.dt.float32
+U32 = mybir.dt.uint32
+U8 = mybir.dt.uint8
+FP8X4 = mybir.dt.float8_e4m3fn_x4
+ALU = mybir.AluOpType
+ACT = mybir.ActivationFunctionType
+AXIS = mybir.AxisListType
+
+P = 128
+PACK = 4
+BANK = 512
+
+ROWS, KEYS, COLS, DIM = 6144, 1024, 512, 128
+ROW_TILES = ROWS // P
+KEY_TILES = KEYS // P
+KEY_BANKS = KEYS // BANK
+KEY_PASSES = KEYS // (P * PACK)
+Q_GROUP = 8
+STORE_GROUP = 4
+
+SCALE = 1.0 / 128.0**0.5
+EPS = 1e-9
+
+FLOPS = 2 * ROWS * (KEYS * DIM + KEYS * COLS + COLS * DIM)
+
+
+def tile_gkatlayer_pa_t_kernel(tc, q, k, counting_attn, v, out):
+    nc = tc.nc
+    with ExitStack() as ctx:
+        const = ctx.enter_context(tc.tile_pool(name="const", bufs=1))
+        work = ctx.enter_context(tc.tile_pool(name="work", bufs=4))
+        psum = ctx.enter_context(tc.psum_pool(name="psum", bufs=1))
+
+        k_rows = const.tile([P, KEY_TILES, DIM], BF16)
+        nc.sync.dma_start(out=k_rows[:], in_=k.rearrange("(a p) d -> p a d", p=P))
+        q_rows = const.tile([P, ROW_TILES, DIM], BF16)
+        q_view = q.rearrange("(p i) d -> p i d", i=ROW_TILES)
+        nc.sync.dma_start(out=q_rows[:, 0:Q_GROUP, :], in_=q_view[:, 0:Q_GROUP, :])
+        c_rows = const.tile([P, KEY_PASSES, PACK, COLS], BF16)
+        nc.sync.dma_start(
+            out=c_rows[:].rearrange("p c (u s) j -> p (c u) (s j)", s=2),
+            in_=counting_attn.rearrange("(g p s) j -> p g (s j)", p=P, s=2),
+        )
+        v_rows = const.tile([P, PACK, DIM], BF16)
+        nc.sync.dma_start(
+            out=v_rows[:].rearrange("p (u s) d -> p u (s d)", s=2),
+            in_=v.rearrange("(u p s) d -> p u (s d)", p=P, s=2),
+        )
+        for g in range(1, ROW_TILES // Q_GROUP):
+            group = slice(g * Q_GROUP, (g + 1) * Q_GROUP)
+            nc.sync.dma_start(out=q_rows[:, group, :], in_=q_view[:, group, :])
+
+        ident_bf16 = const.tile([P, P], BF16)
+        make_identity(nc, ident_bf16[:])
+        ident_f32 = const.tile([P, P], F32)
+        make_identity(nc, ident_f32[:])
+        zero = const.tile([P, 1], F32)
+        nc.vector.memset(zero[:], 0.0)
+        one = const.tile([P, 1], F32)
+        nc.scalar.activation(out=one[:], in_=zero[:], func=ACT.Exp)
+
+        late_banks = ("e_t", "a_nomi", "a_t", "ret")
+
+        def transpose_rows(rows, transposed, n):
+            bank = psum.tile([P, Q_GROUP, P], BF16, name="rows_t", tag=late_banks[n % 4])
+            for a in range(Q_GROUP):
+                nc.tensor.transpose(bank[:, a, :], rows[:, a, :], ident_bf16[:])
+            if n % 2 == 0:
+                nc.vector.tensor_copy(out=transposed, in_=bank[:])
+            else:
+                nc.scalar.copy(out=transposed, in_=bank[:])
+
+        k_t = const.tile([P, KEY_TILES, P], BF16)
+        transpose_rows(k_rows, k_t[:], 0)
+        q_t = const.tile([P, ROW_TILES, P], BF16)
+        for g in range(ROW_TILES // Q_GROUP):
+            group = slice(g * Q_GROUP, (g + 1) * Q_GROUP)
+            transpose_rows(q_rows[:, group, :], q_t[:, group, :], g + 1)
+        k_t_flat = k_t[:].rearrange("p a n -> p (a n)")
+
+        c_grouped = const.tile([P, KEY_PASSES, COLS, PACK], BF16, align_bytes=64)
+        c_codes = const.tile([P, KEY_PASSES, COLS], U32, align_bytes=64)
+        c_scales = const.tile([P, KEY_PASSES, COLS], U8, align_bytes=64)
+        for c in range(KEY_PASSES):
+            nc.vector.tensor_copy(out=c_grouped[:, c], in_=c_rows[:, c].rearrange("p t j -> p j t"))
+        v_grouped = const.tile([P, DIM, PACK], BF16, align_bytes=64)
+        v_codes = const.tile([P, DIM], U32, align_bytes=64)
+        v_scales = const.tile([P, DIM], U8, align_bytes=64)
+        nc.vector.tensor_copy(out=v_grouped[:], in_=v_rows[:].rearrange("p t d -> p d t"))
+        for c in range(KEY_PASSES):
+            nc.vector.quantize_mx(
+                out=c_codes[:, c, :].bitcast(FP8X4),
+                scales=c_scales[:, c, :],
+                in_=c_grouped[:, c].rearrange("p j t -> p (j t)"),
+            )
+        nc.vector.quantize_mx(
+            out=v_codes[:].bitcast(FP8X4),
+            scales=v_scales[:],
+            in_=v_grouped[:].rearrange("p d t -> p (d t)"),
+        )
+
+        out_view = out.rearrange("(p i) d -> p i d", i=ROW_TILES)
+        ret = psum.tile([P, STORE_GROUP, DIM], F32, name="ret", tag="ret")
+        live = {}
+
+        def score(i):
+            for h in range(KEY_BANKS):
+                bank = psum.tile([P, BANK], F32, name="logits%d" % h, tag="logits%d" % h, bufs=2)
+                nc.tensor.matmul(
+                    out=bank[:],
+                    lhsT=q_t[:, i, :],
+                    rhs=k_t_flat[:, h * BANK : (h + 1) * BANK],
+                    start=True,
+                    stop=True,
+                )
+                live["logits", h, i] = bank
+
+        def row_max(i):
+            half_max = work.tile([P, KEY_BANKS], F32, name="half_max")
+            for h in range(KEY_BANKS):
+                nc.vector.reduce_max(
+                    out=half_max[:, h : h + 1], in_=live["logits", h, i][:], axis=AXIS.X
+                )
+            live["half_max", i] = half_max
+
+        def exp_bias(i):
+            half_max = live["half_max", i]
+            bias = work.tile([P, 1], F32, name="bias")
+            nc.vector.tensor_scalar(
+                out=bias[:],
+                in0=half_max[:, 0:1],
+                scalar1=half_max[:, 1:2],
+                scalar2=-SCALE,
+                op0=ALU.max,
+                op1=ALU.mult,
+            )
+            live["bias", i] = bias
+
+        def exponent(i):
+            e = work.tile([P, KEYS], BF16, name="e")
+            for h in range(KEY_BANKS):
+                nc.scalar.activation(
+                    out=e[:, h * BANK : (h + 1) * BANK],
+                    in_=live["logits", h, i][:],
+                    func=ACT.Exp,
+                    bias=live["bias", i][:, 0:1],
+                    scale=SCALE,
+                )
+            live["e", i] = e
+
+        def transpose_e(i):
+            e_words = live["e", i][:].bitcast(F32)
+            e_t = psum.tile([P, KEY_PASSES * 2, P], F32, name="e_t", tag="e_t")
+            for w in range(KEY_PASSES * 2):
+                nc.tensor.transpose(e_t[:, w, :], e_words[:, w * P : (w + 1) * P], ident_f32[:])
+            live["e_t", i] = e_t
+
+        def group_e(i):
+            e_grouped = work.tile([P, KEYS], BF16, name="e_grouped", align_bytes=64)
+            nc.scalar.copy(
+                out=e_grouped[:].bitcast(F32).rearrange("p (c r u) -> p c r u", c=KEY_PASSES, u=2),
+                in_=live["e_t", i][:].rearrange("p (c u) r -> p c r u", u=2),
+            )
+            live["e_grouped", i] = e_grouped
+
+        def quantise_e(i):
+            e_codes = work.tile([P, KEY_PASSES * P], U32, name="e_codes", align_bytes=64)
+            e_scales = work.tile([P, KEY_PASSES * P], U8, name="e_scales", align_bytes=64)
+            nc.vector.quantize_mx(
+                out=e_codes[:].bitcast(FP8X4), scales=e_scales[:], in_=live["e_grouped", i][:]
+            )
+            live["e_codes", i] = e_codes
+            live["e_scales", i] = e_scales
+
+        def weigh(i):
+            a_nomi = psum.tile([P, COLS], F32, name="a_nomi", tag="a_nomi")
+            for c in range(KEY_PASSES):
+                rows_of_pass = slice(c * P, (c + 1) * P)
+                nc.tensor.matmul_mx(
+                    out=a_nomi[:],
+                    lhsT=live["e_codes", i][:, rows_of_pass].bitcast(FP8X4),
+                    lhsT_scale=live["e_scales", i][:, rows_of_pass],
+                    rhs=c_codes[:, c, :].bitcast(FP8X4),
+                    rhs_scale=c_scales[:, c, :],
+                    start=(c == 0),
+                    stop=(c == KEY_PASSES - 1),
+                )
+            live["a_nomi", i] = a_nomi
+
+        def row_sum(i):
+            a_sums = work.tile([P, COLS], F32, name="a_sums")
+            a_deno = work.tile([P, 1], F32, name="a_deno")
+            nc.scalar.activation(
+                out=a_sums[:], in_=live["a_nomi", i][:], func=ACT.Copy, accum_out=a_deno[:]
+            )
+            live["a_sums", i] = a_sums
+            live["a_deno", i] = a_deno
+
+        def add_eps(i):
+            a_deno_eps = work.tile([P, 1], F32, name="a_deno_eps")
+            nc.vector.tensor_scalar_add(out=a_deno_eps[:], in0=live["a_deno", i][:], scalar1=EPS)
+            live["a_deno_eps", i] = a_deno_eps
+
+        def invert(i):
+            a_scale = work.tile([P, 1], F32, name="a_scale")
+            nc.vector.reciprocal(out=a_scale[:], in_=live["a_deno_eps", i][:])
+            live["a_scale", i] = a_scale
+
+        def normalise(i):
+            a_nor = work.tile([P, COLS], BF16, name="a_nor")
+            nc.vector.tensor_scalar_mul(
+                out=a_nor[:], in0=live["a_sums", i][:], scalar1=live["a_scale", i][:, 0:1]
+            )
+            live["a_nor", i] = a_nor
+
+        def transpose_a(i):
+            a_words = live["a_nor", i][:].bitcast(F32)
+            a_t = psum.tile([P, 2, P], F32, name="a_t", tag="a_t")
+            for u in range(2):
+                nc.tensor.transpose(a_t[:, u, :], a_words[:, u * P : (u + 1) * P], ident_f32[:])
+            live["a_t", i] = a_t
+
+        def group_a(i):
+            a_grouped = work.tile([P, COLS], BF16, name="a_grouped", align_bytes=64)
+            nc.vector.tensor_copy(
+                out=a_grouped[:].bitcast(F32).rearrange("p (r u) -> p r u", u=2),
+                in_=live["a_t", i][:].rearrange("p u r -> p r u"),
+            )
+            live["a_grouped", i] = a_grouped
+
+        def quantise_a(i):
+            a_codes = work.tile([P, P], U32, name="a_codes", align_bytes=64)
+            a_scales = work.tile([P, P], U8, name="a_scales", align_bytes=64)
+            nc.vector.quantize_mx(
+                out=a_codes[:].bitcast(FP8X4), scales=a_scales[:], in_=live["a_grouped", i][:]
+            )
+            live["a_codes", i] = a_codes
+            live["a_scales", i] = a_scales
+
+        def project(i):
+            nc.tensor.matmul_mx(
+                out=ret[:, i % STORE_GROUP, :],
+                lhsT=live["a_codes", i][:].bitcast(FP8X4),
+                lhsT_scale=live["a_scales", i][:],
+                rhs=v_codes[:].bitcast(FP8X4),
+                rhs_scale=v_scales[:],
+                start=True,
+                stop=True,
+            )
+
+        def elu_relu(i):
+            relu_minus = work.tile([P, DIM], F32, name="relu_minus")
+            nc.scalar.activation(
+                out=relu_minus[:], in_=ret[:, i % STORE_GROUP, :], func=ACT.Relu, scale=-1.0
+            )
+            live["relu_minus", i] = relu_minus
+
+        def elu_exp(i):
+            exp_low = work.tile([P, DIM], F32, name="exp_low")
+            nc.scalar.activation(
+                out=exp_low[:], in_=live["relu_minus", i][:], func=ACT.Exp, scale=-1.0
+            )
+            live["exp_low", i] = exp_low
+
+        def elu_join(i):
+            place = i % STORE_GROUP
+            if place == 0:
+                live["result"] = work.tile([P, STORE_GROUP, DIM], F32, name="result")
+            result = live["result"]
+            nc.vector.scalar_tensor_tensor(
+                out=result[:, place, :],
+                in0=live["exp_low", i][:],
+                scalar=-1.0,
+                in1=ret[:, place, :],
+                op0=ALU.add,
+                op1=ALU.max,
+            )
+            if place == STORE_GROUP - 1:
+                nc.sync.dma_start(out=out_view[:, i - place : i + 1, :], in_=result[:])
+
+        def at(stage, i):
+            if 0 <= i < ROW_TILES:
+                stage(i)
+
+        with tc.manual_schedule():
+            for j in range(-1, ROW_TILES + 7):
+                at(transpose_a, j - 5)
+                at(row_max, j)
+                at(score, j + 1)
+                at(quantise_a, j - 6)
+                at(exp_bias, j)
+                at(transpose_e, j - 1)
+                at(quantise_e, j - 2)
+                at(exponent, j)
+                at(project, j - 6)
+                at(weigh, j - 2)
+                at(add_eps, j - 4)
+                at(group_a, j - 5)
+                at(invert, j - 4)
+                at(elu_join, j - 7)
+                at(normalise, j - 4)
+                at(group_e, j - 1)
+                at(elu_relu, j - 6)
+                at(row_sum, j - 2)
+                at(elu_exp, j - 6)

@@ -65,45 +65,46 @@ def tile_gkatlayer_pa_t_kernel(tc, q, k, counting_attn, v, out):
         one = const.tile([P, 1], F32)
         nc.scalar.activation(out=one[:], in_=zero[:], func=ACT.Exp)
 
-        late_banks = ("e_t", "a_nomi", "a_t", "ret")
+        k_t = const.tile([P, KEY_TILES, P], BF16)
+        q_t = const.tile([P, ROW_TILES, P], BF16)
+        k_t_flat = k_t[:].rearrange("p a n -> p (a n)")
 
-        def transpose_rows(rows, transposed, n):
-            bank = psum.tile([P, Q_GROUP, P], BF16, name="rows_t", tag=late_banks[n % 4])
+        def transpose_rows(rows, transposed, bank_tag, copy):
+            bank = psum.tile([P, Q_GROUP, P], BF16, name="rows_t", tag=bank_tag)
             for a in range(Q_GROUP):
                 nc.tensor.transpose(bank[:, a, :], rows[:, a, :], ident_bf16[:])
-            if n % 2 == 0:
-                nc.vector.tensor_copy(out=transposed, in_=bank[:])
-            else:
-                nc.scalar.copy(out=transposed, in_=bank[:])
+            copy(out=transposed, in_=bank[:])
 
-        k_t = const.tile([P, KEY_TILES, P], BF16)
-        transpose_rows(k_rows, k_t[:], 0)
-        q_t = const.tile([P, ROW_TILES, P], BF16)
-        for g in range(ROW_TILES // Q_GROUP):
+        def transpose_q(g):
             group = slice(g * Q_GROUP, (g + 1) * Q_GROUP)
-            transpose_rows(q_rows[:, group, :], q_t[:, group, :], g + 1)
-        k_t_flat = k_t[:].rearrange("p a n -> p (a n)")
+            transpose_rows(q_rows[:, group, :], q_t[:, group, :], "a_t", nc.vector.tensor_copy)
 
         c_grouped = const.tile([P, KEY_PASSES, COLS, PACK], BF16, align_bytes=64)
         c_codes = const.tile([P, KEY_PASSES, COLS], U32, align_bytes=64)
         c_scales = const.tile([P, KEY_PASSES, COLS], U8, align_bytes=64)
-        for c in range(KEY_PASSES):
-            nc.vector.tensor_copy(out=c_grouped[:, c], in_=c_rows[:, c].rearrange("p t j -> p j t"))
         v_grouped = const.tile([P, DIM, PACK], BF16, align_bytes=64)
         v_codes = const.tile([P, DIM], U32, align_bytes=64)
         v_scales = const.tile([P, DIM], U8, align_bytes=64)
-        nc.vector.tensor_copy(out=v_grouped[:], in_=v_rows[:].rearrange("p t d -> p d t"))
-        for c in range(KEY_PASSES):
+
+        def group_c(c):
+            nc.vector.tensor_copy(out=c_grouped[:, c], in_=c_rows[:, c].rearrange("p t j -> p j t"))
+
+        def quantise_c(c):
             nc.vector.quantize_mx(
                 out=c_codes[:, c, :].bitcast(FP8X4),
                 scales=c_scales[:, c, :],
                 in_=c_grouped[:, c].rearrange("p j t -> p (j t)"),
             )
-        nc.vector.quantize_mx(
-            out=v_codes[:].bitcast(FP8X4),
-            scales=v_scales[:],
-            in_=v_grouped[:].rearrange("p d t -> p (d t)"),
-        )
+
+        def group_v():
+            nc.vector.tensor_copy(out=v_grouped[:], in_=v_rows[:].rearrange("p t d -> p d t"))
+
+        def quantise_v():
+            nc.vector.quantize_mx(
+                out=v_codes[:].bitcast(FP8X4),
+                scales=v_scales[:],
+                in_=v_grouped[:].rearrange("p d t -> p (d t)"),
+            )
 
         out_view = out.rearrange("(p i) d -> p i d", i=ROW_TILES)
         ret = psum.tile([P, STORE_GROUP, DIM], F32, name="ret", tag="ret")
@@ -214,8 +215,13 @@ def tile_gkatlayer_pa_t_kernel(tc, q, k, counting_attn, v, out):
 
         def normalise(i):
             a_nor = work.tile([P, COLS], BF16, name="a_nor")
-            nc.vector.tensor_scalar_mul(
-                out=a_nor[:], in0=live["a_sums", i][:], scalar1=live["a_scale", i][:, 0:1]
+            nc.gpsimd.tensor_scalar(
+                out=a_nor[:],
+                in0=live["a_sums", i][:],
+                scalar1=live["a_scale", i][:, 0:1],
+                scalar2=0.0,
+                op0=ALU.mult,
+                op1=ALU.add,
             )
             live["a_nor", i] = a_nor
 
@@ -254,18 +260,14 @@ def tile_gkatlayer_pa_t_kernel(tc, q, k, counting_attn, v, out):
                 stop=True,
             )
 
-        def elu_relu(i):
-            relu_minus = work.tile([P, DIM], F32, name="relu_minus")
-            nc.scalar.activation(
-                out=relu_minus[:], in_=ret[:, i % STORE_GROUP, :], func=ACT.Relu, scale=-1.0
-            )
-            live["relu_minus", i] = relu_minus
+        def elu_min(i):
+            low = work.tile([P, DIM], F32, name="low")
+            nc.vector.tensor_scalar_min(out=low[:], in0=ret[:, i % STORE_GROUP, :], scalar1=0.0)
+            live["low", i] = low
 
         def elu_exp(i):
             exp_low = work.tile([P, DIM], F32, name="exp_low")
-            nc.scalar.activation(
-                out=exp_low[:], in_=live["relu_minus", i][:], func=ACT.Exp, scale=-1.0
-            )
+            nc.scalar.activation(out=exp_low[:], in_=live["low", i][:], func=ACT.Exp)
             live["exp_low", i] = exp_low
 
         def elu_join(i):
@@ -284,28 +286,38 @@ def tile_gkatlayer_pa_t_kernel(tc, q, k, counting_attn, v, out):
             if place == STORE_GROUP - 1:
                 nc.sync.dma_start(out=out_view[:, i - place : i + 1, :], in_=result[:])
 
-        def at(stage, i):
-            if 0 <= i < ROW_TILES:
+        def at(stage, i, count=ROW_TILES):
+            if 0 <= i < count:
                 stage(i)
 
         with tc.manual_schedule():
-            for j in range(-1, ROW_TILES + 7):
-                at(transpose_a, j - 5)
+            transpose_rows(k_rows, k_t[:], "e_t", nc.vector.tensor_copy)
+            transpose_rows(q_rows[:, 0:Q_GROUP, :], q_t[:, 0:Q_GROUP, :], "a_nomi", nc.scalar.copy)
+            for j in range(-1, ROW_TILES + 9):
+                at(transpose_a, j - 6)
                 at(row_max, j)
                 at(score, j + 1)
-                at(quantise_a, j - 6)
+                at(quantise_a, j - 7)
                 at(exp_bias, j)
                 at(transpose_e, j - 1)
-                at(quantise_e, j - 2)
                 at(exponent, j)
-                at(project, j - 6)
-                at(weigh, j - 2)
                 at(add_eps, j - 4)
-                at(group_a, j - 5)
+                at(group_a, j - 6)
+                at(group_c, j, KEY_PASSES)
+                at(quantise_c, j - 1, KEY_PASSES)
+                at(quantise_e, j - 2)
+                at(project, j - 7)
+                at(weigh, j - 2)
+                if j == KEY_PASSES:
+                    group_v()
+                if 1 <= j + 1 < ROW_TILES // Q_GROUP:
+                    transpose_q(j + 1)
+                if j == KEY_PASSES + 1:
+                    quantise_v()
                 at(invert, j - 4)
-                at(elu_join, j - 7)
+                at(elu_min, j - 8)
+                at(elu_join, j - 9)
                 at(normalise, j - 4)
                 at(group_e, j - 1)
-                at(elu_relu, j - 6)
                 at(row_sum, j - 2)
-                at(elu_exp, j - 6)
+                at(elu_exp, j - 8)

@@ -23,6 +23,7 @@ KEY_BANKS = KEYS // BANK
 KEY_PASSES = KEYS // (P * PACK)
 Q_GROUP = 8
 STORE_GROUP = 4
+RUN = 4
 
 SCALE = 1.0 / 128.0**0.5
 EPS = 1e-9
@@ -77,7 +78,7 @@ def tile_gkatlayer_pa_t_kernel(tc, q, k, counting_attn, v, out):
 
         def transpose_q(g):
             group = slice(g * Q_GROUP, (g + 1) * Q_GROUP)
-            transpose_rows(q_rows[:, group, :], q_t[:, group, :], "a_t", nc.vector.tensor_copy)
+            transpose_rows(q_rows[:, group, :], q_t[:, group, :], "a_t", nc.scalar.copy)
 
         c_grouped = const.tile([P, KEY_PASSES, COLS, PACK], BF16, align_bytes=64)
         c_codes = const.tile([P, KEY_PASSES, COLS], U32, align_bytes=64)
@@ -87,7 +88,10 @@ def tile_gkatlayer_pa_t_kernel(tc, q, k, counting_attn, v, out):
         v_scales = const.tile([P, DIM], U8, align_bytes=64)
 
         def group_c(c):
-            nc.vector.tensor_copy(out=c_grouped[:, c], in_=c_rows[:, c].rearrange("p t j -> p j t"))
+            nc.vector.tensor_copy(
+                out=c_grouped[:, c].rearrange("p (b i) t -> p b t i", i=RUN),
+                in_=c_rows[:, c].rearrange("p t (b i) -> p b t i", i=RUN),
+            )
 
         def quantise_c(c):
             nc.vector.quantize_mx(
@@ -97,7 +101,10 @@ def tile_gkatlayer_pa_t_kernel(tc, q, k, counting_attn, v, out):
             )
 
         def group_v():
-            nc.vector.tensor_copy(out=v_grouped[:], in_=v_rows[:].rearrange("p t d -> p d t"))
+            nc.vector.tensor_copy(
+                out=v_grouped[:].rearrange("p (b i) t -> p b t i", i=RUN),
+                in_=v_rows[:].rearrange("p t (b i) -> p b t i", i=RUN),
+            )
 
         def quantise_v():
             nc.vector.quantize_mx(

@@ -19,6 +19,7 @@ BANK = 512
 ROWS, KEYS, COLS, DIM = 6144, 1024, 512, 128
 ROW_TILES = ROWS // P
 KEY_TILES = KEYS // P
+HALF_KEYS = KEY_TILES // 2
 KEY_BANKS = KEYS // BANK
 KEY_PASSES = KEYS // (P * PACK)
 Q_GROUP = 8
@@ -39,10 +40,12 @@ def tile_gkatlayer_pa_t_kernel(tc, q, k, counting_attn, v, out):
         psum = ctx.enter_context(tc.psum_pool(name="psum", bufs=1))
 
         k_rows = const.tile([P, KEY_TILES, DIM], BF16)
-        nc.sync.dma_start(out=k_rows[:], in_=k.rearrange("(a p) d -> p a d", p=P))
+        k_view = k.rearrange("(a p) d -> p a d", p=P)
         q_rows = const.tile([P, ROW_TILES, DIM], BF16)
         q_view = q.rearrange("(p i) d -> p i d", i=ROW_TILES)
+        nc.sync.dma_start(out=k_rows[:, 0:HALF_KEYS, :], in_=k_view[:, 0:HALF_KEYS, :])
         nc.sync.dma_start(out=q_rows[:, 0:Q_GROUP, :], in_=q_view[:, 0:Q_GROUP, :])
+        nc.sync.dma_start(out=k_rows[:, HALF_KEYS:, :], in_=k_view[:, HALF_KEYS:, :])
         c_rows = const.tile([P, KEY_PASSES, PACK, COLS], BF16)
         nc.sync.dma_start(
             out=c_rows[:].rearrange("p c (u s) j -> p (c u) (s j)", s=2),
@@ -71,10 +74,11 @@ def tile_gkatlayer_pa_t_kernel(tc, q, k, counting_attn, v, out):
         k_t_flat = k_t[:].rearrange("p a n -> p (a n)")
 
         def transpose_rows(rows, transposed, bank_tag, copy):
+            count = rows.shape[1]
             bank = psum.tile([P, Q_GROUP, P], BF16, name="rows_t", tag=bank_tag)
-            for a in range(Q_GROUP):
+            for a in range(count):
                 nc.tensor.transpose(bank[:, a, :], rows[:, a, :], ident_bf16[:])
-            copy(out=transposed, in_=bank[:])
+            copy(out=transposed, in_=bank[:, 0:count, :])
 
         def transpose_q(g):
             group = slice(g * Q_GROUP, (g + 1) * Q_GROUP)
@@ -169,13 +173,25 @@ def tile_gkatlayer_pa_t_kernel(tc, q, k, counting_attn, v, out):
                 nc.tensor.transpose(e_t[:, w, :], e_words[:, w * P : (w + 1) * P], ident_f32[:])
             live["e_t", i] = e_t
 
+        def scalar_passes(i):
+            return KEY_PASSES - i % 2
+
+        def copy_e(i, copy, passes):
+            copy(
+                out=live["e_grouped", i][:]
+                .bitcast(F32)
+                .rearrange("p (c r u) -> p c r u", c=KEY_PASSES, u=2)[:, passes],
+                in_=live["e_t", i][:].rearrange("p (c u) r -> p c r u", u=2)[:, passes],
+            )
+
         def group_e(i):
             e_grouped = work.tile([P, KEYS], BF16, name="e_grouped", align_bytes=64)
-            nc.scalar.copy(
-                out=e_grouped[:].bitcast(F32).rearrange("p (c r u) -> p c r u", c=KEY_PASSES, u=2),
-                in_=live["e_t", i][:].rearrange("p (c u) r -> p c r u", u=2),
-            )
             live["e_grouped", i] = e_grouped
+            copy_e(i, nc.scalar.copy, slice(0, scalar_passes(i)))
+
+        def group_e_rest(i):
+            if scalar_passes(i) < KEY_PASSES:
+                copy_e(i, nc.vector.tensor_copy, slice(scalar_passes(i), KEY_PASSES))
 
         def quantise_e(i):
             e_codes = work.tile([P, KEY_PASSES * P], U32, name="e_codes", align_bytes=64)
@@ -212,7 +228,14 @@ def tile_gkatlayer_pa_t_kernel(tc, q, k, counting_attn, v, out):
 
         def add_eps(i):
             a_deno_eps = work.tile([P, 1], F32, name="a_deno_eps")
-            nc.vector.tensor_scalar_add(out=a_deno_eps[:], in0=live["a_deno", i][:], scalar1=EPS)
+            nc.gpsimd.tensor_scalar(
+                out=a_deno_eps[:],
+                in0=live["a_deno", i][:],
+                scalar1=1.0,
+                scalar2=EPS,
+                op0=ALU.mult,
+                op1=ALU.add,
+            )
             live["a_deno_eps", i] = a_deno_eps
 
         def invert(i):
@@ -267,15 +290,22 @@ def tile_gkatlayer_pa_t_kernel(tc, q, k, counting_attn, v, out):
                 stop=True,
             )
 
-        def elu_min(i):
-            low = work.tile([P, DIM], F32, name="low")
-            nc.vector.tensor_scalar_min(out=low[:], in0=ret[:, i % STORE_GROUP, :], scalar1=0.0)
-            live["low", i] = low
-
         def elu_exp(i):
-            exp_low = work.tile([P, DIM], F32, name="exp_low")
-            nc.scalar.activation(out=exp_low[:], in_=live["low", i][:], func=ACT.Exp)
-            live["exp_low", i] = exp_low
+            exp_x = work.tile([P, DIM], F32, name="exp_x")
+            nc.scalar.activation(out=exp_x[:], in_=ret[:, i % STORE_GROUP, :], func=ACT.Exp)
+            live["exp_x", i] = exp_x
+
+        def elu_minus_one(i):
+            low = work.tile([P, DIM], F32, name="low")
+            nc.gpsimd.tensor_scalar(
+                out=low[:],
+                in0=live["exp_x", i][:],
+                scalar1=1.0,
+                scalar2=-1.0,
+                op0=ALU.mult,
+                op1=ALU.add,
+            )
+            live["low", i] = low
 
         def elu_join(i):
             place = i % STORE_GROUP
@@ -284,10 +314,10 @@ def tile_gkatlayer_pa_t_kernel(tc, q, k, counting_attn, v, out):
             result = live["result"]
             nc.vector.scalar_tensor_tensor(
                 out=result[:, place, :],
-                in0=live["exp_low", i][:],
-                scalar=-1.0,
+                in0=live["low", i][:],
+                scalar=0.0,
                 in1=ret[:, place, :],
-                op0=ALU.add,
+                op0=ALU.min,
                 op1=ALU.max,
             )
             if place == STORE_GROUP - 1:
@@ -298,33 +328,39 @@ def tile_gkatlayer_pa_t_kernel(tc, q, k, counting_attn, v, out):
                 stage(i)
 
         with tc.manual_schedule():
-            transpose_rows(k_rows, k_t[:], "e_t", nc.vector.tensor_copy)
-            transpose_rows(q_rows[:, 0:Q_GROUP, :], q_t[:, 0:Q_GROUP, :], "a_nomi", nc.scalar.copy)
-            for j in range(-1, ROW_TILES + 9):
-                at(transpose_a, j - 6)
+            low, high = slice(0, HALF_KEYS), slice(HALF_KEYS, KEY_TILES)
+            transpose_rows(k_rows[:, low, :], k_t[:, low, :], "e_t", nc.vector.tensor_copy)
+            transpose_rows(q_rows[:, 0:1, :], q_t[:, 0:1, :], "a_nomi", nc.scalar.copy)
+            transpose_rows(k_rows[:, high, :], k_t[:, high, :], "a_t", nc.vector.tensor_copy)
+            for j in range(-1, ROW_TILES + 10):
+                at(transpose_e, j - 2)
                 at(row_max, j)
+                at(group_e, j - 2)
+                at(weigh, j - 4)
                 at(score, j + 1)
-                at(quantise_a, j - 7)
+                if j == -1:
+                    rest = slice(1, Q_GROUP)
+                    transpose_rows(q_rows[:, rest, :], q_t[:, rest, :], "a_nomi", nc.scalar.copy)
+                at(row_sum, j - 4)
+                at(group_a, j - 7)
+                at(quantise_e, j - 3)
                 at(exp_bias, j)
-                at(transpose_e, j - 1)
-                at(exponent, j)
-                at(add_eps, j - 4)
-                at(group_a, j - 6)
                 at(group_c, j, KEY_PASSES)
                 at(quantise_c, j - 1, KEY_PASSES)
-                at(quantise_e, j - 2)
-                at(project, j - 7)
-                at(weigh, j - 2)
                 if j == KEY_PASSES:
                     group_v()
-                if 1 <= j + 1 < ROW_TILES // Q_GROUP:
-                    transpose_q(j + 1)
                 if j == KEY_PASSES + 1:
                     quantise_v()
-                at(invert, j - 4)
-                at(elu_min, j - 8)
-                at(elu_join, j - 9)
-                at(normalise, j - 4)
-                at(group_e, j - 1)
-                at(row_sum, j - 2)
-                at(elu_exp, j - 8)
+                at(quantise_a, j - 7)
+                at(transpose_a, j - 6)
+                at(invert, j - 5)
+                at(group_e_rest, j - 2)
+                at(elu_join, j - 10)
+                at(project, j - 7)
+                at(exponent, j)
+                if 1 <= j + 1 < ROW_TILES // Q_GROUP:
+                    transpose_q(j + 1)
+                at(elu_exp, j - 7)
+                at(normalise, j - 5)
+                at(add_eps, j - 4)
+                at(elu_minus_one, j - 8)

@@ -333,7 +333,6 @@ def tile_gkatlayer_pa_t_kernel(tc, q, k, counting_attn, v, out):
             transpose_rows(q_rows[:, 0:1, :], q_t[:, 0:1, :], "a_nomi", nc.scalar.copy)
             transpose_rows(k_rows[:, high, :], k_t[:, high, :], "a_t", nc.vector.tensor_copy)
             for j in range(-1, ROW_TILES + 10):
-                at(transpose_e, j - 2)
                 at(row_max, j)
                 at(group_e, j - 2)
                 at(weigh, j - 4)
@@ -355,6 +354,7 @@ def tile_gkatlayer_pa_t_kernel(tc, q, k, counting_attn, v, out):
                 at(transpose_a, j - 6)
                 at(invert, j - 5)
                 at(group_e_rest, j - 2)
+                at(transpose_e, j - 1)
                 at(elu_join, j - 10)
                 at(project, j - 7)
                 at(exponent, j)

@@ -26,6 +26,8 @@ Q_GROUP = 8
 STORE_GROUP = 4
 RUN = 4
 
+LAST = 4
+
 SCALE = 1.0 / 128.0**0.5
 EPS = 1e-9
 
@@ -44,8 +46,9 @@ def tile_gkatlayer_pa_t_kernel(tc, q, k, counting_attn, v, out):
         q_rows = const.tile([P, ROW_TILES, DIM], BF16)
         q_view = q.rearrange("(p i) d -> p i d", i=ROW_TILES)
         nc.sync.dma_start(out=k_rows[:, 0:HALF_KEYS, :], in_=k_view[:, 0:HALF_KEYS, :])
-        nc.sync.dma_start(out=q_rows[:, 0:Q_GROUP, :], in_=q_view[:, 0:Q_GROUP, :])
+        nc.sync.dma_start(out=q_rows[:, 0:1, :], in_=q_view[:, 0:1, :])
         nc.sync.dma_start(out=k_rows[:, HALF_KEYS:, :], in_=k_view[:, HALF_KEYS:, :])
+        nc.sync.dma_start(out=q_rows[:, 1:Q_GROUP, :], in_=q_view[:, 1:Q_GROUP, :])
         c_rows = const.tile([P, KEY_PASSES, PACK, COLS], BF16)
         nc.sync.dma_start(
             out=c_rows[:].rearrange("p c (u s) j -> p (c u) (s j)", s=2),
@@ -91,10 +94,15 @@ def tile_gkatlayer_pa_t_kernel(tc, q, k, counting_attn, v, out):
         v_codes = const.tile([P, DIM], U32, align_bytes=64)
         v_scales = const.tile([P, DIM], U8, align_bytes=64)
 
-        def group_c(c):
-            nc.vector.tensor_copy(
+        def group_c(c, copy):
+            copy(
                 out=c_grouped[:, c].rearrange("p (b i) t -> p b t i", i=RUN),
                 in_=c_rows[:, c].rearrange("p t (b i) -> p b t i", i=RUN),
+            )
+
+        def gpsimd_copy(out, in_):
+            nc.gpsimd.tensor_scalar(
+                out=out, in0=in_, scalar1=1.0, scalar2=0.0, op0=ALU.mult, op1=ALU.add
             )
 
         def quantise_c(c):
@@ -105,7 +113,7 @@ def tile_gkatlayer_pa_t_kernel(tc, q, k, counting_attn, v, out):
             )
 
         def group_v():
-            nc.vector.tensor_copy(
+            gpsimd_copy(
                 out=v_grouped[:].rearrange("p (b i) t -> p b t i", i=RUN),
                 in_=v_rows[:].rearrange("p t (b i) -> p b t i", i=RUN),
             )
@@ -172,6 +180,7 @@ def tile_gkatlayer_pa_t_kernel(tc, q, k, counting_attn, v, out):
             for w in range(KEY_PASSES * 2):
                 nc.tensor.transpose(e_t[:, w, :], e_words[:, w * P : (w + 1) * P], ident_f32[:])
             live["e_t", i] = e_t
+            live["e_grouped", i] = work.tile([P, KEYS], BF16, name="e_grouped", align_bytes=64)
 
         def scalar_passes(i):
             return KEY_PASSES - i % 2
@@ -185,8 +194,6 @@ def tile_gkatlayer_pa_t_kernel(tc, q, k, counting_attn, v, out):
             )
 
         def group_e(i):
-            e_grouped = work.tile([P, KEYS], BF16, name="e_grouped", align_bytes=64)
-            live["e_grouped", i] = e_grouped
             copy_e(i, nc.scalar.copy, slice(0, scalar_passes(i)))
 
         def group_e_rest(i):
@@ -217,6 +224,9 @@ def tile_gkatlayer_pa_t_kernel(tc, q, k, counting_attn, v, out):
                 )
             live["a_nomi", i] = a_nomi
 
+        def helper(i):
+            return nc.vector if i >= ROW_TILES - LAST else nc.gpsimd
+
         def row_sum(i):
             a_sums = work.tile([P, COLS], F32, name="a_sums")
             a_deno = work.tile([P, 1], F32, name="a_deno")
@@ -245,7 +255,7 @@ def tile_gkatlayer_pa_t_kernel(tc, q, k, counting_attn, v, out):
 
         def normalise(i):
             a_nor = work.tile([P, COLS], BF16, name="a_nor")
-            nc.gpsimd.tensor_scalar(
+            helper(i).tensor_scalar(
                 out=a_nor[:],
                 in0=live["a_sums", i][:],
                 scalar1=live["a_scale", i][:, 0:1],
@@ -297,7 +307,7 @@ def tile_gkatlayer_pa_t_kernel(tc, q, k, counting_attn, v, out):
 
         def elu_minus_one(i):
             low = work.tile([P, DIM], F32, name="low")
-            nc.gpsimd.tensor_scalar(
+            helper(i).tensor_scalar(
                 out=low[:],
                 in0=live["exp_x", i][:],
                 scalar1=1.0,
@@ -331,9 +341,12 @@ def tile_gkatlayer_pa_t_kernel(tc, q, k, counting_attn, v, out):
             low, high = slice(0, HALF_KEYS), slice(HALF_KEYS, KEY_TILES)
             transpose_rows(k_rows[:, low, :], k_t[:, low, :], "e_t", nc.vector.tensor_copy)
             transpose_rows(q_rows[:, 0:1, :], q_t[:, 0:1, :], "a_nomi", nc.scalar.copy)
-            transpose_rows(k_rows[:, high, :], k_t[:, high, :], "a_t", nc.vector.tensor_copy)
+            transpose_rows(k_rows[:, high, :], k_t[:, high, :], "a_t", nc.scalar.copy)
             for j in range(-1, ROW_TILES + 10):
                 at(row_max, j)
+                at(group_a, j - 7)
+                at(group_e_rest, j - 2)
+                at(exp_bias, j)
                 at(group_e, j - 2)
                 at(weigh, j - 4)
                 at(score, j + 1)
@@ -341,20 +354,22 @@ def tile_gkatlayer_pa_t_kernel(tc, q, k, counting_attn, v, out):
                     rest = slice(1, Q_GROUP)
                     transpose_rows(q_rows[:, rest, :], q_t[:, rest, :], "a_nomi", nc.scalar.copy)
                 at(row_sum, j - 4)
-                at(group_a, j - 7)
-                at(quantise_e, j - 3)
-                at(exp_bias, j)
-                at(group_c, j, KEY_PASSES)
-                at(quantise_c, j - 1, KEY_PASSES)
-                if j == KEY_PASSES:
+                if j == 2:
+                    group_c(0, nc.vector.tensor_copy)
+                if j == -1:
+                    group_c(1, gpsimd_copy)
                     group_v()
-                if j == KEY_PASSES + 1:
+                if j == 3:
+                    quantise_c(0)
+                if j == 3:
+                    quantise_c(1)
+                if j == 4:
                     quantise_v()
+                at(quantise_e, j - 3)
                 at(quantise_a, j - 7)
                 at(transpose_a, j - 6)
-                at(invert, j - 5)
-                at(group_e_rest, j - 2)
                 at(transpose_e, j - 1)
+                at(invert, j - 5)
                 at(elu_join, j - 10)
                 at(project, j - 7)
                 at(exponent, j)

@@ -46,9 +46,9 @@ def tile_gkatlayer_pa_t_kernel(tc, q, k, counting_attn, v, out):
         q_rows = const.tile([P, ROW_TILES, DIM], BF16)
         q_view = q.rearrange("(p i) d -> p i d", i=ROW_TILES)
         nc.sync.dma_start(out=k_rows[:, 0:HALF_KEYS, :], in_=k_view[:, 0:HALF_KEYS, :])
-        nc.sync.dma_start(out=q_rows[:, 0:1, :], in_=q_view[:, 0:1, :])
+        nc.sync.dma_start(out=q_rows[:, 0:2, :], in_=q_view[:, 0:2, :])
         nc.sync.dma_start(out=k_rows[:, HALF_KEYS:, :], in_=k_view[:, HALF_KEYS:, :])
-        nc.sync.dma_start(out=q_rows[:, 1:Q_GROUP, :], in_=q_view[:, 1:Q_GROUP, :])
+        nc.sync.dma_start(out=q_rows[:, 2:Q_GROUP, :], in_=q_view[:, 2:Q_GROUP, :])
         c_rows = const.tile([P, KEY_PASSES, PACK, COLS], BF16)
         nc.sync.dma_start(
             out=c_rows[:].rearrange("p c (u s) j -> p (c u) (s j)", s=2),
@@ -67,6 +67,8 @@ def tile_gkatlayer_pa_t_kernel(tc, q, k, counting_attn, v, out):
         make_identity(nc, ident_bf16[:])
         ident_f32 = const.tile([P, P], F32)
         make_identity(nc, ident_f32[:])
+        idle = const.tile([P, BANK], BF16)
+        nc.vector.memset(idle[:], 0.0)
         zero = const.tile([P, 1], F32)
         nc.vector.memset(zero[:], 0.0)
         one = const.tile([P, 1], F32)
@@ -128,6 +130,16 @@ def tile_gkatlayer_pa_t_kernel(tc, q, k, counting_attn, v, out):
         out_view = out.rearrange("(p i) d -> p i d", i=ROW_TILES)
         ret = psum.tile([P, STORE_GROUP, DIM], F32, name="ret", tag="ret")
         live = {}
+
+        def keep_warm(count):
+            for unused in range(count):
+                nc.tensor.matmul(
+                    out=ret[:].rearrange("p i d -> p (i d)"),
+                    lhsT=idle[:, 0:P],
+                    rhs=idle[:],
+                    start=True,
+                    stop=True,
+                )
 
         def score(i):
             for h in range(KEY_BANKS):
@@ -330,17 +342,20 @@ def tile_gkatlayer_pa_t_kernel(tc, q, k, counting_attn, v, out):
                 op0=ALU.min,
                 op1=ALU.max,
             )
-            if place == STORE_GROUP - 1:
-                nc.sync.dma_start(out=out_view[:, i - place : i + 1, :], in_=result[:])
+            if i >= ROW_TILES - STORE_GROUP // 2:
+                nc.sync.dma_start(out=out_view[:, i : i + 1, :], in_=result[:, place : place + 1, :])
+            elif place == STORE_GROUP - 1 or i == ROW_TILES - STORE_GROUP // 2 - 1:
+                nc.sync.dma_start(out=out_view[:, i - place : i + 1, :], in_=result[:, 0 : place + 1, :])
 
         def at(stage, i, count=ROW_TILES):
             if 0 <= i < count:
                 stage(i)
 
         with tc.manual_schedule():
+            keep_warm(3)
             low, high = slice(0, HALF_KEYS), slice(HALF_KEYS, KEY_TILES)
             transpose_rows(k_rows[:, low, :], k_t[:, low, :], "e_t", nc.vector.tensor_copy)
-            transpose_rows(q_rows[:, 0:1, :], q_t[:, 0:1, :], "a_nomi", nc.scalar.copy)
+            transpose_rows(q_rows[:, 0:2, :], q_t[:, 0:2, :], "a_nomi", nc.scalar.copy)
             transpose_rows(k_rows[:, high, :], k_t[:, high, :], "a_t", nc.scalar.copy)
             for j in range(-1, ROW_TILES + 10):
                 at(row_max, j)
@@ -350,8 +365,10 @@ def tile_gkatlayer_pa_t_kernel(tc, q, k, counting_attn, v, out):
                 at(group_e, j - 2)
                 at(weigh, j - 4)
                 at(score, j + 1)
+                if 0 <= j < 6:
+                    keep_warm(1)
                 if j == -1:
-                    rest = slice(1, Q_GROUP)
+                    rest = slice(2, Q_GROUP)
                     transpose_rows(q_rows[:, rest, :], q_t[:, rest, :], "a_nomi", nc.scalar.copy)
                 at(row_sum, j - 4)
                 if j == 2:
@@ -373,8 +390,8 @@ def tile_gkatlayer_pa_t_kernel(tc, q, k, counting_attn, v, out):
                 at(elu_join, j - 10)
                 at(project, j - 7)
                 at(exponent, j)
-                if 1 <= j + 1 < ROW_TILES // Q_GROUP:
-                    transpose_q(j + 1)
+                if 1 <= j < ROW_TILES // Q_GROUP:
+                    transpose_q(j)
                 at(elu_exp, j - 7)
                 at(normalise, j - 5)
                 at(add_eps, j - 4)

@@ -87,7 +87,16 @@ def tile_gkatlayer_pa_t_kernel(tc, q, k, counting_attn, v, out):
 
         def transpose_q(g):
             group = slice(g * Q_GROUP, (g + 1) * Q_GROUP)
-            transpose_rows(q_rows[:, group, :], q_t[:, group, :], "a_t", nc.scalar.copy)
+            if g in [1]:
+                live["q_bank"] = psum.tile([P, Q_GROUP, P], BF16, name="rows_t", tag="a_t")
+                for a in range(Q_GROUP):
+                    nc.tensor.transpose(live["q_bank"][:, a, :], q_rows[:, group, :][:, a, :], ident_bf16[:])
+            else:
+                transpose_rows(q_rows[:, group, :], q_t[:, group, :], "a_t", nc.scalar.copy)
+
+        def copy_q(g):
+            if g in [1]:
+                nc.vector.tensor_copy(out=q_t[:, g * Q_GROUP : (g + 1) * Q_GROUP, :], in_=live["q_bank"][:])
 
         c_grouped = const.tile([P, KEY_PASSES, COLS, PACK], BF16, align_bytes=64)
         c_codes = const.tile([P, KEY_PASSES, COLS], U32, align_bytes=64)
@@ -195,7 +204,7 @@ def tile_gkatlayer_pa_t_kernel(tc, q, k, counting_attn, v, out):
             live["e_grouped", i] = work.tile([P, KEYS], BF16, name="e_grouped", align_bytes=64)
 
         def scalar_passes(i):
-            return KEY_PASSES - i % 2
+            return KEY_PASSES - (1 if i % 2 or i > 44 else 0)
 
         def copy_e(i, copy, passes):
             copy(
@@ -362,6 +371,8 @@ def tile_gkatlayer_pa_t_kernel(tc, q, k, counting_attn, v, out):
                 at(group_a, j - 7)
                 at(group_e_rest, j - 2)
                 at(exp_bias, j)
+                if 1 <= j - 1 < ROW_TILES // Q_GROUP:
+                    copy_q(j - 1)
                 at(group_e, j - 2)
                 at(weigh, j - 4)
                 at(score, j + 1)
@@ -371,16 +382,15 @@ def tile_gkatlayer_pa_t_kernel(tc, q, k, counting_attn, v, out):
                     rest = slice(2, Q_GROUP)
                     transpose_rows(q_rows[:, rest, :], q_t[:, rest, :], "a_nomi", nc.scalar.copy)
                 at(row_sum, j - 4)
-                if j == 2:
-                    group_c(0, nc.vector.tensor_copy)
                 if j == -1:
+                    group_c(0, gpsimd_copy)
                     group_c(1, gpsimd_copy)
                     group_v()
                 if j == 3:
                     quantise_c(0)
                 if j == 3:
                     quantise_c(1)
-                if j == 4:
+                if j == 5:
                     quantise_v()
                 at(quantise_e, j - 3)
                 at(quantise_a, j - 7)

@@ -50,9 +50,14 @@ def tile_gkatlayer_pa_t_kernel(tc, q, k, counting_attn, v, out):
         nc.sync.dma_start(out=k_rows[:, HALF_KEYS:, :], in_=k_view[:, HALF_KEYS:, :])
         nc.sync.dma_start(out=q_rows[:, 2:Q_GROUP, :], in_=q_view[:, 2:Q_GROUP, :])
         c_rows = const.tile([P, KEY_PASSES, PACK, COLS], BF16)
+        c_view = counting_attn.rearrange("(g p s) j -> p g (s j)", p=P, s=2)
         nc.sync.dma_start(
-            out=c_rows[:].rearrange("p c (u s) j -> p (c u) (s j)", s=2),
-            in_=counting_attn.rearrange("(g p s) j -> p g (s j)", p=P, s=2),
+            out=c_rows[:, 0].rearrange("p (u s) j -> p u (s j)", s=2),
+            in_=c_view[:, 2 * 0 : 2 * 0 + 2, :],
+        )
+        nc.sync.dma_start(
+            out=c_rows[:, 1].rearrange("p (u s) j -> p u (s j)", s=2),
+            in_=c_view[:, 2 * 1 : 2 * 1 + 2, :],
         )
         v_rows = const.tile([P, PACK, DIM], BF16)
         nc.sync.dma_start(
@@ -87,7 +92,7 @@ def tile_gkatlayer_pa_t_kernel(tc, q, k, counting_attn, v, out):
 
         def transpose_q(g):
             group = slice(g * Q_GROUP, (g + 1) * Q_GROUP)
-            if g in [1]:
+            if g in [1, 3, 5]:
                 live["q_bank"] = psum.tile([P, Q_GROUP, P], BF16, name="rows_t", tag="a_t")
                 for a in range(Q_GROUP):
                     nc.tensor.transpose(live["q_bank"][:, a, :], q_rows[:, group, :][:, a, :], ident_bf16[:])
@@ -95,7 +100,7 @@ def tile_gkatlayer_pa_t_kernel(tc, q, k, counting_attn, v, out):
                 transpose_rows(q_rows[:, group, :], q_t[:, group, :], "a_t", nc.scalar.copy)
 
         def copy_q(g):
-            if g in [1]:
+            if g in [1, 3, 5]:
                 nc.vector.tensor_copy(out=q_t[:, g * Q_GROUP : (g + 1) * Q_GROUP, :], in_=live["q_bank"][:])
 
         c_grouped = const.tile([P, KEY_PASSES, COLS, PACK], BF16, align_bytes=64)
@@ -376,8 +381,6 @@ def tile_gkatlayer_pa_t_kernel(tc, q, k, counting_attn, v, out):
                 at(group_e, j - 2)
                 at(weigh, j - 4)
                 at(score, j + 1)
-                if 0 <= j < 6:
-                    keep_warm(1)
                 if j == -1:
                     rest = slice(2, Q_GROUP)
                     transpose_rows(q_rows[:, rest, :], q_t[:, rest, :], "a_nomi", nc.scalar.copy)

@@ -112,8 +112,7 @@ def tile_gkatlayer_pa_t_kernel(tc, q, k, counting_attn, v, out):
 
         def group_c(c, copy):
             copy(
-                out=c_grouped[:, c].rearrange("p (b i) t -> p b t i", i=RUN),
-                in_=c_rows[:, c].rearrange("p t (b i) -> p b t i", i=RUN),
+                out=c_grouped[:, c], in_=c_rows[:, c].rearrange("p t j -> p j t")
             )
 
         def gpsimd_copy(out, in_):
@@ -130,8 +129,7 @@ def tile_gkatlayer_pa_t_kernel(tc, q, k, counting_attn, v, out):
 
         def group_v():
             gpsimd_copy(
-                out=v_grouped[:].rearrange("p (b i) t -> p b t i", i=RUN),
-                in_=v_rows[:].rearrange("p t (b i) -> p b t i", i=RUN),
+                out=v_grouped[:], in_=v_rows[:].rearrange("p t d -> p d t")
             )
 
         def quantise_v():

from contextlib import ExitStack

import concourse.mybir as mybir
from concourse.masks import make_identity

BF16 = mybir.dt.bfloat16
F32 = mybir.dt.float32
U32 = mybir.dt.uint32
U8 = mybir.dt.uint8
FP8X4 = mybir.dt.float8_e4m3fn_x4
ALU = mybir.AluOpType
ACT = mybir.ActivationFunctionType
AXIS = mybir.AxisListType

P = 128
PACK = 4
BANK = 512

ROWS, KEYS, COLS, DIM = 6144, 1024, 512, 128
ROW_TILES = ROWS // P
KEY_TILES = KEYS // P
HALF_KEYS = KEY_TILES // 2
KEY_BANKS = KEYS // BANK
KEY_PASSES = KEYS // (P * PACK)
Q_GROUP = 8
STORE_GROUP = 4
RUN = 4

LAST = 4

SCALE = 1.0 / 128.0**0.5
EPS = 1e-9

FLOPS = 2 * ROWS * (KEYS * DIM + KEYS * COLS + COLS * DIM)


def tile_gkatlayer_pa_t_kernel(tc, q, k, counting_attn, v, out):
    nc = tc.nc
    with ExitStack() as ctx:
        const = ctx.enter_context(tc.tile_pool(name="const", bufs=1))
        work = ctx.enter_context(tc.tile_pool(name="work", bufs=4))
        psum = ctx.enter_context(tc.psum_pool(name="psum", bufs=1))

        k_rows = const.tile([P, KEY_TILES, DIM], BF16)
        k_view = k.rearrange("(a p) d -> p a d", p=P)
        q_rows = const.tile([P, ROW_TILES, DIM], BF16)
        q_view = q.rearrange("(p i) d -> p i d", i=ROW_TILES)
        nc.sync.dma_start(out=k_rows[:, 0:HALF_KEYS, :], in_=k_view[:, 0:HALF_KEYS, :])
        nc.sync.dma_start(out=q_rows[:, 0:2, :], in_=q_view[:, 0:2, :])
        nc.sync.dma_start(out=k_rows[:, HALF_KEYS:, :], in_=k_view[:, HALF_KEYS:, :])
        nc.sync.dma_start(out=q_rows[:, 2:Q_GROUP, :], in_=q_view[:, 2:Q_GROUP, :])
        c_rows = const.tile([P, KEY_PASSES, PACK, COLS], BF16)
        c_view = counting_attn.rearrange("(g p s) j -> p g (s j)", p=P, s=2)
        nc.sync.dma_start(
            out=c_rows[:, 0].rearrange("p (u s) j -> p u (s j)", s=2),
            in_=c_view[:, 2 * 0 : 2 * 0 + 2, :],
        )
        nc.sync.dma_start(
            out=c_rows[:, 1].rearrange("p (u s) j -> p u (s j)", s=2),
            in_=c_view[:, 2 * 1 : 2 * 1 + 2, :],
        )
        v_rows = const.tile([P, PACK, DIM], BF16)
        nc.sync.dma_start(
            out=v_rows[:].rearrange("p (u s) d -> p u (s d)", s=2),
            in_=v.rearrange("(u p s) d -> p u (s d)", p=P, s=2),
        )
        for g in range(1, ROW_TILES // Q_GROUP):
            group = slice(g * Q_GROUP, (g + 1) * Q_GROUP)
            nc.sync.dma_start(out=q_rows[:, group, :], in_=q_view[:, group, :])

        ident_bf16 = const.tile([P, P], BF16)
        make_identity(nc, ident_bf16[:])
        ident_f32 = const.tile([P, P], F32)
        make_identity(nc, ident_f32[:])
        idle = const.tile([P, BANK], BF16)
        nc.vector.memset(idle[:], 0.0)
        zero = const.tile([P, 1], F32)
        nc.vector.memset(zero[:], 0.0)
        one = const.tile([P, 1], F32)
        nc.scalar.activation(out=one[:], in_=zero[:], func=ACT.Exp)

        k_t = const.tile([P, KEY_TILES, P], BF16)
        q_t = const.tile([P, ROW_TILES, P], BF16)
        k_t_flat = k_t[:].rearrange("p a n -> p (a n)")

        def transpose_rows(rows, transposed, bank_tag, copy):
            count = rows.shape[1]
            bank = psum.tile([P, Q_GROUP, P], BF16, name="rows_t", tag=bank_tag)
            for a in range(count):
                nc.tensor.transpose(bank[:, a, :], rows[:, a, :], ident_bf16[:])
            copy(out=transposed, in_=bank[:, 0:count, :])

        def transpose_q(g):
            group = slice(g * Q_GROUP, (g + 1) * Q_GROUP)
            if g in [1, 3, 5]:
                live["q_bank"] = psum.tile([P, Q_GROUP, P], BF16, name="rows_t", tag="a_t")
                for a in range(Q_GROUP):
                    nc.tensor.transpose(live["q_bank"][:, a, :], q_rows[:, group, :][:, a, :], ident_bf16[:])
            else:
                transpose_rows(q_rows[:, group, :], q_t[:, group, :], "a_t", nc.scalar.copy)

        def copy_q(g):
            if g in [1, 3, 5]:
                nc.vector.tensor_copy(out=q_t[:, g * Q_GROUP : (g + 1) * Q_GROUP, :], in_=live["q_bank"][:])

        c_grouped = const.tile([P, KEY_PASSES, COLS, PACK], BF16, align_bytes=64)
        c_codes = const.tile([P, KEY_PASSES, COLS], U32, align_bytes=64)
        c_scales = const.tile([P, KEY_PASSES, COLS], U8, align_bytes=64)
        v_grouped = const.tile([P, DIM, PACK], BF16, align_bytes=64)
        v_codes = const.tile([P, DIM], U32, align_bytes=64)
        v_scales = const.tile([P, DIM], U8, align_bytes=64)

        def group_c(c, copy):
            copy(
                out=c_grouped[:, c], in_=c_rows[:, c].rearrange("p t j -> p j t")
            )

        def gpsimd_copy(out, in_):
            nc.gpsimd.tensor_scalar(
                out=out, in0=in_, scalar1=1.0, scalar2=0.0, op0=ALU.mult, op1=ALU.add
            )

        def quantise_c(c):
            nc.vector.quantize_mx(
                out=c_codes[:, c, :].bitcast(FP8X4),
                scales=c_scales[:, c, :],
                in_=c_grouped[:, c].rearrange("p j t -> p (j t)"),
            )

        def group_v():
            gpsimd_copy(
                out=v_grouped[:], in_=v_rows[:].rearrange("p t d -> p d t")
            )

        def quantise_v():
            nc.vector.quantize_mx(
                out=v_codes[:].bitcast(FP8X4),
                scales=v_scales[:],
                in_=v_grouped[:].rearrange("p d t -> p (d t)"),
            )

        out_view = out.rearrange("(p i) d -> p i d", i=ROW_TILES)
        ret = psum.tile([P, STORE_GROUP, DIM], F32, name="ret", tag="ret")
        live = {}

        def keep_warm(count):
            for unused in range(count):
                nc.tensor.matmul(
                    out=ret[:].rearrange("p i d -> p (i d)"),
                    lhsT=idle[:, 0:P],
                    rhs=idle[:],
                    start=True,
                    stop=True,
                )

        def score(i):
            for h in range(KEY_BANKS):
                bank = psum.tile([P, BANK], F32, name="logits%d" % h, tag="logits%d" % h, bufs=2)
                nc.tensor.matmul(
                    out=bank[:],
                    lhsT=q_t[:, i, :],
                    rhs=k_t_flat[:, h * BANK : (h + 1) * BANK],
                    start=True,
                    stop=True,
                )
                live["logits", h, i] = bank

        def row_max(i):
            half_max = work.tile([P, KEY_BANKS], F32, name="half_max")
            for h in range(KEY_BANKS):
                nc.vector.reduce_max(
                    out=half_max[:, h : h + 1], in_=live["logits", h, i][:], axis=AXIS.X
                )
            live["half_max", i] = half_max

        def exp_bias(i):
            half_max = live["half_max", i]
            bias = work.tile([P, 1], F32, name="bias")
            nc.vector.tensor_scalar(
                out=bias[:],
                in0=half_max[:, 0:1],
                scalar1=half_max[:, 1:2],
                scalar2=-SCALE,
                op0=ALU.max,
                op1=ALU.mult,
            )
            live["bias", i] = bias

        def exponent(i):
            e = work.tile([P, KEYS], BF16, name="e")
            for h in range(KEY_BANKS):
                nc.scalar.activation(
                    out=e[:, h * BANK : (h + 1) * BANK],
                    in_=live["logits", h, i][:],
                    func=ACT.Exp,
                    bias=live["bias", i][:, 0:1],
                    scale=SCALE,
                )
            live["e", i] = e

        def transpose_e(i):
            e_words = live["e", i][:].bitcast(F32)
            e_t = psum.tile([P, KEY_PASSES * 2, P], F32, name="e_t", tag="e_t")
            for w in range(KEY_PASSES * 2):
                nc.tensor.transpose(e_t[:, w, :], e_words[:, w * P : (w + 1) * P], ident_f32[:])
            live["e_t", i] = e_t
            live["e_grouped", i] = work.tile([P, KEYS], BF16, name="e_grouped", align_bytes=64)

        def scalar_passes(i):
            return KEY_PASSES - (1 if i % 2 or i > 44 else 0)

        def copy_e(i, copy, passes):
            copy(
                out=live["e_grouped", i][:]
                .bitcast(F32)
                .rearrange("p (c r u) -> p c r u", c=KEY_PASSES, u=2)[:, passes],
                in_=live["e_t", i][:].rearrange("p (c u) r -> p c r u", u=2)[:, passes],
            )

        def group_e(i):
            copy_e(i, nc.scalar.copy, slice(0, scalar_passes(i)))

        def group_e_rest(i):
            if scalar_passes(i) < KEY_PASSES:
                copy_e(i, nc.vector.tensor_copy, slice(scalar_passes(i), KEY_PASSES))

        def quantise_e(i):
            e_codes = work.tile([P, KEY_PASSES * P], U32, name="e_codes", align_bytes=64)
            e_scales = work.tile([P, KEY_PASSES * P], U8, name="e_scales", align_bytes=64)
            nc.vector.quantize_mx(
                out=e_codes[:].bitcast(FP8X4), scales=e_scales[:], in_=live["e_grouped", i][:]
            )
            live["e_codes", i] = e_codes
            live["e_scales", i] = e_scales

        def weigh(i):
            a_nomi = psum.tile([P, COLS], F32, name="a_nomi", tag="a_nomi")
            for c in range(KEY_PASSES):
                rows_of_pass = slice(c * P, (c + 1) * P)
                nc.tensor.matmul_mx(
                    out=a_nomi[:],
                    lhsT=live["e_codes", i][:, rows_of_pass].bitcast(FP8X4),
                    lhsT_scale=live["e_scales", i][:, rows_of_pass],
                    rhs=c_codes[:, c, :].bitcast(FP8X4),
                    rhs_scale=c_scales[:, c, :],
                    start=(c == 0),
                    stop=(c == KEY_PASSES - 1),
                )
            live["a_nomi", i] = a_nomi

        def helper(i):
            return nc.vector if i >= ROW_TILES - LAST else nc.gpsimd

        def row_sum(i):
            a_sums = work.tile([P, COLS], F32, name="a_sums")
            a_deno = work.tile([P, 1], F32, name="a_deno")
            nc.scalar.activation(
                out=a_sums[:], in_=live["a_nomi", i][:], func=ACT.Copy, accum_out=a_deno[:]
            )
            live["a_sums", i] = a_sums
            live["a_deno", i] = a_deno

        def add_eps(i):
            a_deno_eps = work.tile([P, 1], F32, name="a_deno_eps")
            nc.gpsimd.tensor_scalar(
                out=a_deno_eps[:],
                in0=live["a_deno", i][:],
                scalar1=1.0,
                scalar2=EPS,
                op0=ALU.mult,
                op1=ALU.add,
            )
            live["a_deno_eps", i] = a_deno_eps

        def invert(i):
            a_scale = work.tile([P, 1], F32, name="a_scale")
            nc.vector.reciprocal(out=a_scale[:], in_=live["a_deno_eps", i][:])
            live["a_scale", i] = a_scale

        def normalise(i):
            a_nor = work.tile([P, COLS], BF16, name="a_nor")
            helper(i).tensor_scalar(
                out=a_nor[:],
                in0=live["a_sums", i][:],
                scalar1=live["a_scale", i][:, 0:1],
                scalar2=0.0,
                op0=ALU.mult,
                op1=ALU.add,
            )
            live["a_nor", i] = a_nor

        def transpose_a(i):
            a_words = live["a_nor", i][:].bitcast(F32)
            a_t = psum.tile([P, 2, P], F32, name="a_t", tag="a_t")
            for u in range(2):
                nc.tensor.transpose(a_t[:, u, :], a_words[:, u * P : (u + 1) * P], ident_f32[:])
            live["a_t", i] = a_t

        def group_a(i):
            a_grouped = work.tile([P, COLS], BF16, name="a_grouped", align_bytes=64)
            nc.vector.tensor_copy(
                out=a_grouped[:].bitcast(F32).rearrange("p (r u) -> p r u", u=2),
                in_=live["a_t", i][:].rearrange("p u r -> p r u"),
            )
            live["a_grouped", i] = a_grouped

        def quantise_a(i):
            a_codes = work.tile([P, P], U32, name="a_codes", align_bytes=64)
            a_scales = work.tile([P, P], U8, name="a_scales", align_bytes=64)
            nc.vector.quantize_mx(
                out=a_codes[:].bitcast(FP8X4), scales=a_scales[:], in_=live["a_grouped", i][:]
            )
            live["a_codes", i] = a_codes
            live["a_scales", i] = a_scales

        def project(i):
            nc.tensor.matmul_mx(
                out=ret[:, i % STORE_GROUP, :],
                lhsT=live["a_codes", i][:].bitcast(FP8X4),
                lhsT_scale=live["a_scales", i][:],
                rhs=v_codes[:].bitcast(FP8X4),
                rhs_scale=v_scales[:],
                start=True,
                stop=True,
            )

        def elu_exp(i):
            exp_x = work.tile([P, DIM], F32, name="exp_x")
            nc.scalar.activation(out=exp_x[:], in_=ret[:, i % STORE_GROUP, :], func=ACT.Exp)
            live["exp_x", i] = exp_x

        def elu_minus_one(i):
            low = work.tile([P, DIM], F32, name="low")
            helper(i).tensor_scalar(
                out=low[:],
                in0=live["exp_x", i][:],
                scalar1=1.0,
                scalar2=-1.0,
                op0=ALU.mult,
                op1=ALU.add,
            )
            live["low", i] = low

        def elu_join(i):
            place = i % STORE_GROUP
            if place == 0:
                live["result"] = work.tile([P, STORE_GROUP, DIM], F32, name="result")
            result = live["result"]
            nc.vector.scalar_tensor_tensor(
                out=result[:, place, :],
                in0=live["low", i][:],
                scalar=0.0,
                in1=ret[:, place, :],
                op0=ALU.min,
                op1=ALU.max,
            )
            if i >= ROW_TILES - STORE_GROUP // 2:
                nc.sync.dma_start(out=out_view[:, i : i + 1, :], in_=result[:, place : place + 1, :])
            elif place == STORE_GROUP - 1 or i == ROW_TILES - STORE_GROUP // 2 - 1:
                nc.sync.dma_start(out=out_view[:, i - place : i + 1, :], in_=result[:, 0 : place + 1, :])

        def at(stage, i, count=ROW_TILES):
            if 0 <= i < count:
                stage(i)

        with tc.manual_schedule():
            keep_warm(3)
            low, high = slice(0, HALF_KEYS), slice(HALF_KEYS, KEY_TILES)
            transpose_rows(k_rows[:, low, :], k_t[:, low, :], "e_t", nc.vector.tensor_copy)
            transpose_rows(q_rows[:, 0:2, :], q_t[:, 0:2, :], "a_nomi", nc.scalar.copy)
            transpose_rows(k_rows[:, high, :], k_t[:, high, :], "a_t", nc.scalar.copy)
            for j in range(-1, ROW_TILES + 10):
                at(row_max, j)
                at(group_a, j - 7)
                at(group_e_rest, j - 2)
                at(exp_bias, j)
                if 1 <= j - 1 < ROW_TILES // Q_GROUP:
                    copy_q(j - 1)
                at(group_e, j - 2)
                at(weigh, j - 4)
                at(score, j + 1)
                if j == -1:
                    rest = slice(2, Q_GROUP)
                    transpose_rows(q_rows[:, rest, :], q_t[:, rest, :], "a_nomi", nc.scalar.copy)
                at(row_sum, j - 4)
                if j == -1:
                    group_c(0, gpsimd_copy)
                    group_c(1, gpsimd_copy)
                    group_v()
                if j == 3:
                    quantise_c(0)
                if j == 3:
                    quantise_c(1)
                if j == 5:
                    quantise_v()
                at(quantise_e, j - 3)
                at(quantise_a, j - 7)
                at(transpose_a, j - 6)
                at(transpose_e, j - 1)
                at(invert, j - 5)
                at(elu_join, j - 10)
                at(project, j - 7)
                at(exponent, j)
                if 1 <= j < ROW_TILES // Q_GROUP:
                    transpose_q(j)
                at(elu_exp, j - 7)
                at(normalise, j - 5)
                at(add_eps, j - 4)
                at(elu_minus_one, j - 8)
